import numpy as np
import ml_dtypes

BF16 = ml_dtypes.bfloat16


def bf(x):
    return np.asarray(x, np.float32).astype(BF16)


def f32(x):
    return np.asarray(x, np.float32)


def f64(x):
    return np.asarray(x).astype(np.float64)


def striped(idx):
    return np.tile(idx.reshape(-1, 16).T, (8, 1))


V, E, H, K, O, N = 4096, 128, 256, 2, 512, 512
SIB_SCALE = 1.0 / np.sqrt(H)
EPS = 1e-8


def setup_inputs():
    return {"table": bf(np.random.standard_normal((V, E))), "w": bf(np.random.standard_normal((E, H)) / np.sqrt(E)), "proj_b": f32(0.1 * np.random.standard_normal((H, 1))), "child_w": bf(np.random.standard_normal((H, H)) / np.sqrt(H)), "child_b": f32(0.1 * np.random.standard_normal((H, 1))), "sib_emb": f32(np.random.standard_normal((H, K))), "head_w": bf(np.random.standard_normal((H, O)) / np.sqrt(H)), "head_b": f32(0.1 * np.random.standard_normal((O, 1))), "offs": striped(np.random.permutation(np.tile(np.arange(V), 2))[:N])}


def reference(table, w, proj_b, child_w, child_b, sib_emb, head_w, head_b, offs):
    idx = offs[:16].T.reshape(-1)
    h = f64(w).T @ f64(table)[idx].T + f64(proj_b)
    t = np.tanh(f64(child_w).T @ h + f64(child_b))
    total = h + K * t + SIB_SCALE * f64(sib_emb).sum(axis=1, keepdims=True)
    pooled = total / (1 + K + EPS)
    return f64(head_w).T @ pooled + f64(head_b)

@@ -1,0 +1,110 @@
+from contextlib import ExitStack
+
+import concourse.mybir as mybir
+from concourse.masks import make_identity
+
+V, E, H, O, N = 4096, 128, 256, 512, 512
+P = 128
+FLOPS = 2 * N * (E * H + H * H + H * O)
+
+BF16, F32, U16 = mybir.dt.bfloat16, mybir.dt.float32, mybir.dt.uint16
+ADD, MULT = mybir.AluOpType.add, mybir.AluOpType.mult
+FUNC = mybir.ActivationFunctionType
+
+HALVES = H // P
+OUT_BLOCKS = O // P
+BANK = 1024
+CHUNKS = V // BANK
+BLOCKS = BANK // P
+MEAN = 1.0 / (3.0 + 1e-8)
+
+
+def tile_boenet_kernel(tc, table, w, proj_b, child_w, child_b, sib_emb, head_w, head_b, offs, out):
+    nc = tc.nc
+    with ExitStack() as ctx:
+        held = ctx.enter_context(tc.tile_pool(name="held", bufs=1))
+        work = ctx.enter_context(tc.tile_pool(name="work", bufs=2))
+        psum = ctx.enter_context(tc.psum_pool(name="psum", bufs=2))
+
+        offsets = held.tile([P, N // 16], U16, name="offsets")
+        nc.sync.dma_start(offsets[:], offs)
+
+        rows = []
+        for c in range(CHUNKS):
+            chunk = held.tile([P, BLOCKS, E], BF16, name=f"rows{c}")
+            queue = nc.sync if c % 2 == 0 else nc.scalar
+            queue.dma_start(chunk[:], table[c * BANK : (c + 1) * BANK, :].rearrange("(b p) e -> p b e", p=P))
+            rows.append(chunk)
+
+        w_sb = held.tile([P, H], BF16, name="w_sb")
+        nc.sync.dma_start(w_sb[:], w)
+        child_sb = held.tile([P, HALVES, H], BF16, name="child_sb")
+        nc.scalar.dma_start(child_sb[:], child_w.rearrange("(a p) m -> p a m", p=P))
+        head_sb = held.tile([P, HALVES, O], BF16, name="head_sb")
+        nc.sync.dma_start(head_sb[:], head_w.rearrange("(a p) o -> p a o", p=P))
+
+        proj_bias = held.tile([P, HALVES], F32, name="proj_bias")
+        child_bias = held.tile([P, HALVES], F32, name="child_bias")
+        siblings = held.tile([P, HALVES, 2], F32, name="siblings")
+        head_bias = held.tile([P, OUT_BLOCKS], F32, name="head_bias")
+        with nc.allow_non_contiguous_dma(reason="bias vectors, one element to a partition"):
+            nc.gpsimd.dma_start(proj_bias[:], proj_b.rearrange("(a p) x -> p (a x)", p=P))
+            nc.gpsimd.dma_start(siblings[:], sib_emb.rearrange("(a p) k -> p a k", p=P))
+            nc.gpsimd.dma_start(child_bias[:], child_b.rearrange("(a p) x -> p (a x)", p=P))
+            nc.gpsimd.dma_start(head_bias[:], head_b.rearrange("(a p) x -> p (a x)", p=P))
+
+        identity = held.tile([P, P], BF16, name="identity")
+        make_identity(nc, identity[:])
+
+        warm = held.tile([P, 1], F32, name="warm")
+        nc.vector.memset(warm[:], 0.0)
+        nc.scalar.activation(warm[:], warm[:], FUNC.Tanh)
+
+        root_bias = held.tile([P, HALVES], F32, name="root_bias")
+        nc.vector.tensor_tensor(root_bias[:], siblings[:, :, 0], siblings[:, :, 1], ADD)
+        nc.vector.scalar_tensor_tensor(root_bias[:], root_bias[:], 1.0 / 16.0, proj_bias[:], MULT, ADD)
+        nc.vector.tensor_scalar(root_bias[:], root_bias[:], MEAN, None, MULT)
+
+        window = held.tile([P, V], BF16, name="window")
+        for c in range(CHUNKS):
+            flipped = psum.tile([P, BANK], BF16, name="flipped")
+            for b in range(BLOCKS):
+                nc.tensor.transpose(flipped[:, b * P : (b + 1) * P], rows[c][:, b, :], identity[:])
+            if c % 2 == 0:
+                nc.vector.tensor_copy(window[:, c * BANK : (c + 1) * BANK], flipped[:])
+            else:
+                nc.scalar.copy(window[:, c * BANK : (c + 1) * BANK], flipped[:])
+
+        root_bf = []
+        root_part = []
+        for a in range(HALVES):
+            root_ps = psum.tile([P, N], F32, name="root_ps")
+            nc.tensor.matmul(root_ps[:], w_sb[:, a * P : (a + 1) * P], window[:].indirect(offsets[:]), start=True, stop=True)
+            h_bf = work.tile([P, N], BF16, name=f"h_bf{a}", bufs=1)
+            nc.vector.tensor_scalar(h_bf[:], root_ps[:], proj_bias[:, a : a + 1], None, ADD)
+            h_part = work.tile([P, N], F32, name=f"h_part{a}", bufs=1)
+            nc.scalar.activation(h_part[:], root_ps[:], FUNC.Identity, bias=root_bias[:, a : a + 1], scale=MEAN)
+            root_bf.append(h_bf)
+            root_part.append(h_part)
+
+        pooled = []
+        for m in range(HALVES):
+            child_ps = psum.tile([P, N], F32, name="child_ps")
+            for a in range(HALVES):
+                nc.tensor.matmul(child_ps[:], child_sb[:, a, m * P : (m + 1) * P], root_bf[a][:], start=(a == 0), stop=(a == HALVES - 1))
+            child = work.tile([P, N], F32, name="child")
+            nc.scalar.activation(child[:], child_ps[:], FUNC.Tanh, bias=child_bias[:, m : m + 1])
+            mean_bf = work.tile([P, N], BF16, name=f"mean_bf{m}", bufs=1)
+            nc.vector.scalar_tensor_tensor(mean_bf[:], child[:], 2.0 * MEAN, root_part[m][:], MULT, ADD)
+            pooled.append(mean_bf)
+
+        for o in range(OUT_BLOCKS):
+            head_ps = psum.tile([P, N], F32, name="head_ps")
+            for m in range(HALVES):
+                nc.tensor.matmul(head_ps[:], head_sb[:, m, o * P : (o + 1) * P], pooled[m][:], start=(m == 0), stop=(m == HALVES - 1))
+            logits = work.tile([P, N], F32, name="logits", bufs=4)
+            if o % 2 == 0:
+                nc.vector.tensor_scalar(logits[:], head_ps[:], head_bias[:, o : o + 1], None, ADD)
+            else:
+                nc.scalar.activation(logits[:], head_ps[:], FUNC.Identity, bias=head_bias[:, o : o + 1])
+            nc.sync.dma_start(out[o * P : (o + 1) * P, :], logits[:])

@@ -26,6 +26,9 @@ def tile_boenet_kernel(tc, table, w, proj_b, child_w, child_b, sib_emb, head_w, 
         work = ctx.enter_context(tc.tile_pool(name="work", bufs=2))
         psum = ctx.enter_context(tc.psum_pool(name="psum", bufs=2))
 
+        identity = held.tile([P, P], BF16, name="identity")
+        make_identity(nc, identity[:])
+
         offsets = held.tile([P, N // 16], U16, name="offsets")
         nc.sync.dma_start(offsets[:], offs)
 
@@ -36,34 +39,31 @@ def tile_boenet_kernel(tc, table, w, proj_b, child_w, child_b, sib_emb, head_w, 
             queue.dma_start(chunk[:], table[c * BANK : (c + 1) * BANK, :].rearrange("(b p) e -> p b e", p=P))
             rows.append(chunk)
 
-        w_sb = held.tile([P, H], BF16, name="w_sb")
-        nc.sync.dma_start(w_sb[:], w)
-        child_sb = held.tile([P, HALVES, H], BF16, name="child_sb")
-        nc.scalar.dma_start(child_sb[:], child_w.rearrange("(a p) m -> p a m", p=P))
-        head_sb = held.tile([P, HALVES, O], BF16, name="head_sb")
-        nc.sync.dma_start(head_sb[:], head_w.rearrange("(a p) o -> p a o", p=P))
-
         proj_bias = held.tile([P, HALVES], F32, name="proj_bias")
-        child_bias = held.tile([P, HALVES], F32, name="child_bias")
         siblings = held.tile([P, HALVES, 2], F32, name="siblings")
+        w_sb = held.tile([P, H], BF16, name="w_sb")
+        child_sb = held.tile([P, HALVES, H], BF16, name="child_sb")
+        child_bias = held.tile([P, HALVES], F32, name="child_bias")
+        head_sb = held.tile([P, HALVES, O], BF16, name="head_sb")
         head_bias = held.tile([P, OUT_BLOCKS], F32, name="head_bias")
         with nc.allow_non_contiguous_dma(reason="bias vectors, one element to a partition"):
-            nc.gpsimd.dma_start(proj_bias[:], proj_b.rearrange("(a p) x -> p (a x)", p=P))
-            nc.gpsimd.dma_start(siblings[:], sib_emb.rearrange("(a p) k -> p a k", p=P))
-            nc.gpsimd.dma_start(child_bias[:], child_b.rearrange("(a p) x -> p (a x)", p=P))
-            nc.gpsimd.dma_start(head_bias[:], head_b.rearrange("(a p) x -> p (a x)", p=P))
-
-        identity = held.tile([P, P], BF16, name="identity")
-        make_identity(nc, identity[:])
+            nc.sync.dma_start(proj_bias[:], proj_b.rearrange("(a p) x -> p (a x)", p=P))
+            nc.sync.dma_start(siblings[:], sib_emb.rearrange("(a p) k -> p a k", p=P))
+            nc.sync.dma_start(w_sb[:], w)
+            nc.sync.dma_start(child_sb[:], child_w.rearrange("(a p) m -> p a m", p=P))
+            nc.sync.dma_start(child_bias[:], child_b.rearrange("(a p) x -> p (a x)", p=P))
+            nc.sync.dma_start(head_sb[:], head_w.rearrange("(a p) o -> p a o", p=P))
+            nc.sync.dma_start(head_bias[:], head_b.rearrange("(a p) x -> p (a x)", p=P))
 
         warm = held.tile([P, 1], F32, name="warm")
         nc.vector.memset(warm[:], 0.0)
         nc.scalar.activation(warm[:], warm[:], FUNC.Tanh)
 
         root_bias = held.tile([P, HALVES], F32, name="root_bias")
-        nc.vector.tensor_tensor(root_bias[:], siblings[:, :, 0], siblings[:, :, 1], ADD)
-        nc.vector.scalar_tensor_tensor(root_bias[:], root_bias[:], 1.0 / 16.0, proj_bias[:], MULT, ADD)
-        nc.vector.tensor_scalar(root_bias[:], root_bias[:], MEAN, None, MULT)
+        nc.gpsimd.tensor_tensor(root_bias[:], siblings[:, :, 0], siblings[:, :, 1], ADD)
+        nc.gpsimd.tensor_scalar(root_bias[:], root_bias[:], 1.0 / 16.0, None, MULT)
+        nc.gpsimd.tensor_tensor(root_bias[:], root_bias[:], proj_bias[:], ADD)
+        nc.gpsimd.tensor_scalar(root_bias[:], root_bias[:], MEAN, None, MULT)
 
         window = held.tile([P, V], BF16, name="window")
         for c in range(CHUNKS):

@@ -15,7 +15,7 @@ HALVES = H // P
 OUT_BLOCKS = O // P
 BANK = 1024
 CHUNKS = V // BANK
-BLOCKS = BANK // P
+RUN = BANK // P
 MEAN = 1.0 / (3.0 + 1e-8)
 
 
@@ -34,9 +34,9 @@ def tile_boenet_kernel(tc, table, w, proj_b, child_w, child_b, sib_emb, head_w, 
 
         rows = []
         for c in range(CHUNKS):
-            chunk = held.tile([P, BLOCKS, E], BF16, name=f"rows{c}")
+            chunk = held.tile([P, RUN, E], BF16, name=f"rows{c}")
             queue = nc.sync if c % 2 == 0 else nc.scalar
-            queue.dma_start(chunk[:], table[c * BANK : (c + 1) * BANK, :].rearrange("(b p) e -> p b e", p=P))
+            queue.dma_start(chunk[:], table[c * BANK : (c + 1) * BANK, :].rearrange("(p r) e -> p r e", r=RUN))
             rows.append(chunk)
 
         proj_bias = held.tile([P, HALVES], F32, name="proj_bias")
@@ -67,13 +67,14 @@ def tile_boenet_kernel(tc, table, w, proj_b, child_w, child_b, sib_emb, head_w, 
 
         window = held.tile([P, V], BF16, name="window")
         for c in range(CHUNKS):
-            flipped = psum.tile([P, BANK], BF16, name="flipped")
-            for b in range(BLOCKS):
-                nc.tensor.transpose(flipped[:, b * P : (b + 1) * P], rows[c][:, b, :], identity[:])
+            flipped = psum.tile([P, RUN, P], BF16, name="flipped")
+            for r in range(RUN):
+                nc.tensor.transpose(flipped[:, r, :], rows[c][:, r, :], identity[:])
+            in_order = window[:, c * BANK : (c + 1) * BANK].rearrange("e (p r) -> e p r", r=RUN)
             if c % 2 == 0:
-                nc.vector.tensor_copy(window[:, c * BANK : (c + 1) * BANK], flipped[:])
+                nc.vector.tensor_copy(in_order, flipped[:].rearrange("e r p -> e p r"))
             else:
-                nc.scalar.copy(window[:, c * BANK : (c + 1) * BANK], flipped[:])
+                nc.scalar.copy(in_order, flipped[:].rearrange("e r p -> e p r"))
 
         root_bf = []
         root_part = []

@@ -16,6 +16,8 @@ OUT_BLOCKS = O // P
 BANK = 1024
 CHUNKS = V // BANK
 RUN = BANK // P
+PIECE = 256
+PIECES = N // PIECE
 MEAN = 1.0 / (3.0 + 1e-8)
 
 
@@ -23,8 +25,8 @@ def tile_boenet_kernel(tc, table, w, proj_b, child_w, child_b, sib_emb, head_w, 
     nc = tc.nc
     with ExitStack() as ctx:
         held = ctx.enter_context(tc.tile_pool(name="held", bufs=1))
-        work = ctx.enter_context(tc.tile_pool(name="work", bufs=2))
-        psum = ctx.enter_context(tc.psum_pool(name="psum", bufs=2))
+        work = ctx.enter_context(tc.tile_pool(name="work", bufs=1))
+        psum = ctx.enter_context(tc.psum_pool(name="psum", bufs=8))
 
         identity = held.tile([P, P], BF16, name="identity")
         make_identity(nc, identity[:])
@@ -67,7 +69,7 @@ def tile_boenet_kernel(tc, table, w, proj_b, child_w, child_b, sib_emb, head_w, 
 
         window = held.tile([P, V], BF16, name="window")
         for c in range(CHUNKS):
-            flipped = psum.tile([P, RUN, P], BF16, name="flipped")
+            flipped = psum.tile([P, RUN, P], BF16, name="flipped", tag="bank")
             for r in range(RUN):
                 nc.tensor.transpose(flipped[:, r, :], rows[c][:, r, :], identity[:])
             in_order = window[:, c * BANK : (c + 1) * BANK].rearrange("e (p r) -> e p r", r=RUN)
@@ -76,36 +78,45 @@ def tile_boenet_kernel(tc, table, w, proj_b, child_w, child_b, sib_emb, head_w, 
             else:
                 nc.scalar.copy(in_order, flipped[:].rearrange("e r p -> e p r"))
 
-        root_bf = []
-        root_part = []
-        for a in range(HALVES):
-            root_ps = psum.tile([P, N], F32, name="root_ps")
-            nc.tensor.matmul(root_ps[:], w_sb[:, a * P : (a + 1) * P], window[:].indirect(offsets[:]), start=True, stop=True)
-            h_bf = work.tile([P, N], BF16, name=f"h_bf{a}", bufs=1)
-            nc.vector.tensor_scalar(h_bf[:], root_ps[:], proj_bias[:, a : a + 1], None, ADD)
-            h_part = work.tile([P, N], F32, name=f"h_part{a}", bufs=1)
-            nc.scalar.activation(h_part[:], root_ps[:], FUNC.Identity, bias=root_bias[:, a : a + 1], scale=MEAN)
-            root_bf.append(h_bf)
-            root_part.append(h_part)
 
-        pooled = []
-        for m in range(HALVES):
-            child_ps = psum.tile([P, N], F32, name="child_ps")
+        root_bf = {}
+        root_part = {}
+        for j in range(PIECES):
             for a in range(HALVES):
-                nc.tensor.matmul(child_ps[:], child_sb[:, a, m * P : (m + 1) * P], root_bf[a][:], start=(a == 0), stop=(a == HALVES - 1))
-            child = work.tile([P, N], F32, name="child")
-            nc.scalar.activation(child[:], child_ps[:], FUNC.Tanh, bias=child_bias[:, m : m + 1])
-            mean_bf = work.tile([P, N], BF16, name=f"mean_bf{m}", bufs=1)
-            nc.vector.scalar_tensor_tensor(mean_bf[:], child[:], 2.0 * MEAN, root_part[m][:], MULT, ADD)
-            pooled.append(mean_bf)
+                looked_up = window[:].indirect(offsets[:, j * PIECE // 16 : (j + 1) * PIECE // 16])
+                root_ps = psum.tile([P, PIECE], F32, name="root_ps", tag="bank")
+                nc.tensor.matmul(root_ps[:], w_sb[:, a * P : (a + 1) * P], looked_up, start=True, stop=True)
+                h_bf = work.tile([P, PIECE], BF16, name=f"h_bf_{a}_{j}")
+                h_part = work.tile([P, PIECE], F32, name=f"h_part_{a}_{j}")
+                if a == 0:
+                    nc.vector.tensor_scalar(h_bf[:], root_ps[:], proj_bias[:, a : a + 1], None, ADD)
+                    nc.vector.tensor_scalar(h_part[:], root_ps[:], MEAN, root_bias[:, a : a + 1], MULT, ADD)
+                else:
+                    nc.scalar.activation(h_bf[:], root_ps[:], FUNC.Identity, bias=proj_bias[:, a : a + 1])
+                    nc.scalar.activation(h_part[:], root_ps[:], FUNC.Identity, bias=root_bias[:, a : a + 1], scale=MEAN)
+                root_bf[a, j] = h_bf
+                root_part[a, j] = h_part
 
-        for o in range(OUT_BLOCKS):
-            head_ps = psum.tile([P, N], F32, name="head_ps")
+        pooled = {}
+        for j in range(PIECES):
             for m in range(HALVES):
-                nc.tensor.matmul(head_ps[:], head_sb[:, m, o * P : (o + 1) * P], pooled[m][:], start=(m == 0), stop=(m == HALVES - 1))
-            logits = work.tile([P, N], F32, name="logits", bufs=4)
-            if o % 2 == 0:
-                nc.vector.tensor_scalar(logits[:], head_ps[:], head_bias[:, o : o + 1], None, ADD)
-            else:
-                nc.scalar.activation(logits[:], head_ps[:], FUNC.Identity, bias=head_bias[:, o : o + 1])
-            nc.sync.dma_start(out[o * P : (o + 1) * P, :], logits[:])
+                child_ps = psum.tile([P, PIECE], F32, name="child_ps", tag="bank")
+                for a in range(HALVES):
+                    nc.tensor.matmul(child_ps[:], child_sb[:, a, m * P : (m + 1) * P], root_bf[a, j][:], start=(a == 0), stop=(a == HALVES - 1))
+                child = work.tile([P, PIECE], F32, name=f"child_{m}_{j}")
+                nc.scalar.activation(child[:], child_ps[:], FUNC.Tanh, bias=child_bias[:, m : m + 1])
+                mean_bf = work.tile([P, PIECE], BF16, name=f"mean_bf_{m}_{j}")
+                nc.vector.scalar_tensor_tensor(mean_bf[:], child[:], 2.0 * MEAN, root_part[m, j][:], MULT, ADD)
+                pooled[m, j] = mean_bf
+
+        for j in range(PIECES):
+            for o in range(OUT_BLOCKS):
+                head_ps = psum.tile([P, PIECE], F32, name="head_ps", tag="bank")
+                for m in range(HALVES):
+                    nc.tensor.matmul(head_ps[:], head_sb[:, m, o * P : (o + 1) * P], pooled[m, j][:], start=(m == 0), stop=(m == HALVES - 1))
+                logits = work.tile([P, PIECE], F32, name=f"logits_{o}_{j}")
+                if o % 2 == 0:
+                    nc.vector.tensor_scalar(logits[:], head_ps[:], head_bias[:, o : o + 1], None, ADD)
+                else:
+                    nc.scalar.activation(logits[:], head_ps[:], FUNC.Identity, bias=head_bias[:, o : o + 1])
+                nc.sync.dma_start(out[o * P : (o + 1) * P, j * PIECE : (j + 1) * PIECE], logits[:])

@@ -13,9 +13,9 @@ FUNC = mybir.ActivationFunctionType
 
 HALVES = H // P
 OUT_BLOCKS = O // P
-BANK = 1024
-CHUNKS = V // BANK
-RUN = BANK // P
+CHUNK = 512
+CHUNKS = V // CHUNK
+RUN = CHUNK // P
 PIECE = 256
 PIECES = N // PIECE
 MEAN = 1.0 / (3.0 + 1e-8)
@@ -31,15 +31,15 @@ def tile_boenet_kernel(tc, table, w, proj_b, child_w, child_b, sib_emb, head_w, 
         identity = held.tile([P, P], BF16, name="identity")
         make_identity(nc, identity[:])
 
-        offsets = held.tile([P, N // 16], U16, name="offsets")
-        nc.sync.dma_start(offsets[:], offs)
-
         rows = []
         for c in range(CHUNKS):
             chunk = held.tile([P, RUN, E], BF16, name=f"rows{c}")
             queue = nc.sync if c % 2 == 0 else nc.scalar
-            queue.dma_start(chunk[:], table[c * BANK : (c + 1) * BANK, :].rearrange("(p r) e -> p r e", r=RUN))
+            queue.dma_start(chunk[:], table[c * CHUNK : (c + 1) * CHUNK, :].rearrange("(p r) e -> p r e", r=RUN))
             rows.append(chunk)
+
+        offsets = held.tile([P, N // 16], U16, name="offsets")
+        nc.sync.dma_start(offsets[:], offs)
 
         proj_bias = held.tile([P, HALVES], F32, name="proj_bias")
         siblings = held.tile([P, HALVES, 2], F32, name="siblings")
@@ -72,7 +72,7 @@ def tile_boenet_kernel(tc, table, w, proj_b, child_w, child_b, sib_emb, head_w, 
             flipped = psum.tile([P, RUN, P], BF16, name="flipped", tag="bank")
             for r in range(RUN):
                 nc.tensor.transpose(flipped[:, r, :], rows[c][:, r, :], identity[:])
-            in_order = window[:, c * BANK : (c + 1) * BANK].rearrange("e (p r) -> e p r", r=RUN)
+            in_order = window[:, c * CHUNK : (c + 1) * CHUNK].rearrange("e (p r) -> e p r", r=RUN)
             if c % 2 == 0:
                 nc.vector.tensor_copy(in_order, flipped[:].rearrange("e r p -> e p r"))
             else:

@@ -18,6 +18,7 @@ CHUNKS = V // CHUNK
 RUN = CHUNK // P
 PIECE = 256
 PIECES = N // PIECE
+WARM_UP = 4
 MEAN = 1.0 / (3.0 + 1e-8)
 
 
@@ -26,10 +27,16 @@ def tile_boenet_kernel(tc, table, w, proj_b, child_w, child_b, sib_emb, head_w, 
     with ExitStack() as ctx:
         held = ctx.enter_context(tc.tile_pool(name="held", bufs=1))
         work = ctx.enter_context(tc.tile_pool(name="work", bufs=1))
-        psum = ctx.enter_context(tc.psum_pool(name="psum", bufs=8))
+        psum = ctx.enter_context(tc.psum_pool(name="psum", bufs=7))
 
         identity = held.tile([P, P], BF16, name="identity")
         make_identity(nc, identity[:])
+
+        unread_ps = psum.tile([P, N], F32, name="unread_ps", bufs=1)
+        zeros = held.tile([P, N], BF16, name="zeros")
+        nc.vector.memset(zeros[:], 0.0)
+        for i in range(WARM_UP):
+            nc.tensor.matmul(unread_ps[:], zeros[:, 0:P], zeros[:], start=True, stop=True)
 
         rows = []
         for c in range(CHUNKS):
@@ -77,6 +84,7 @@ def tile_boenet_kernel(tc, table, w, proj_b, child_w, child_b, sib_emb, head_w, 
                 nc.vector.tensor_copy(in_order, flipped[:].rearrange("e r p -> e p r"))
             else:
                 nc.scalar.copy(in_order, flipped[:].rearrange("e r p -> e p r"))
+                nc.tensor.matmul(unread_ps[:], identity[:], rows[c][:].rearrange("p r e -> p (r e)"), start=True, stop=True)
 
 
         root_bf = {}

@@ -15,7 +15,7 @@ HALVES = H // P
 OUT_BLOCKS = O // P
 CHUNK = 512
 CHUNKS = V // CHUNK
-RUN = CHUNK // P
+BLOCKS = CHUNK // P
 PIECE = 256
 PIECES = N // PIECE
 WARM_UP = 4
@@ -40,9 +40,9 @@ def tile_boenet_kernel(tc, table, w, proj_b, child_w, child_b, sib_emb, head_w, 
 
         rows = []
         for c in range(CHUNKS):
-            chunk = held.tile([P, RUN, E], BF16, name=f"rows{c}")
+            chunk = held.tile([P, BLOCKS, E], BF16, name=f"rows{c}")
             queue = nc.sync if c % 2 == 0 else nc.scalar
-            queue.dma_start(chunk[:], table[c * CHUNK : (c + 1) * CHUNK, :].rearrange("(p r) e -> p r e", r=RUN))
+            queue.dma_start(chunk[:], table[c * CHUNK : (c + 1) * CHUNK, :].rearrange("(b p) e -> p b e", p=P))
             rows.append(chunk)
 
         offsets = held.tile([P, N // 16], U16, name="offsets")
@@ -76,15 +76,14 @@ def tile_boenet_kernel(tc, table, w, proj_b, child_w, child_b, sib_emb, head_w, 
 
         window = held.tile([P, V], BF16, name="window")
         for c in range(CHUNKS):
-            flipped = psum.tile([P, RUN, P], BF16, name="flipped", tag="bank")
-            for r in range(RUN):
-                nc.tensor.transpose(flipped[:, r, :], rows[c][:, r, :], identity[:])
-            in_order = window[:, c * CHUNK : (c + 1) * CHUNK].rearrange("e (p r) -> e p r", r=RUN)
+            flipped = psum.tile([P, CHUNK], BF16, name="flipped", tag="bank")
+            for b in range(BLOCKS):
+                nc.tensor.transpose(flipped[:, b * P : (b + 1) * P], rows[c][:, b, :], identity[:])
             if c % 2 == 0:
-                nc.vector.tensor_copy(in_order, flipped[:].rearrange("e r p -> e p r"))
+                nc.vector.tensor_copy(window[:, c * CHUNK : (c + 1) * CHUNK], flipped[:])
             else:
-                nc.scalar.copy(in_order, flipped[:].rearrange("e r p -> e p r"))
-                nc.tensor.matmul(unread_ps[:], identity[:], rows[c][:].rearrange("p r e -> p (r e)"), start=True, stop=True)
+                nc.scalar.copy(window[:, c * CHUNK : (c + 1) * CHUNK], flipped[:])
+                nc.tensor.matmul(unread_ps[:], identity[:], rows[c][:].rearrange("p b e -> p (b e)"), start=True, stop=True)
 
 
         root_bf = {}

@@ -15,7 +15,7 @@ HALVES = H // P
 OUT_BLOCKS = O // P
 CHUNK = 512
 CHUNKS = V // CHUNK
-BLOCKS = CHUNK // P
+RUN = CHUNK // P
 PIECE = 256
 PIECES = N // PIECE
 WARM_UP = 4
@@ -40,9 +40,9 @@ def tile_boenet_kernel(tc, table, w, proj_b, child_w, child_b, sib_emb, head_w, 
 
         rows = []
         for c in range(CHUNKS):
-            chunk = held.tile([P, BLOCKS, E], BF16, name=f"rows{c}")
+            chunk = held.tile([P, RUN, E], BF16, name=f"rows{c}")
             queue = nc.sync if c % 2 == 0 else nc.scalar
-            queue.dma_start(chunk[:], table[c * CHUNK : (c + 1) * CHUNK, :].rearrange("(b p) e -> p b e", p=P))
+            queue.dma_start(chunk[:], table[c * CHUNK : (c + 1) * CHUNK, :].rearrange("(p r) e -> p r e", r=RUN))
             rows.append(chunk)
 
         offsets = held.tile([P, N // 16], U16, name="offsets")
@@ -76,14 +76,15 @@ def tile_boenet_kernel(tc, table, w, proj_b, child_w, child_b, sib_emb, head_w, 
 
         window = held.tile([P, V], BF16, name="window")
         for c in range(CHUNKS):
-            flipped = psum.tile([P, CHUNK], BF16, name="flipped", tag="bank")
-            for b in range(BLOCKS):
-                nc.tensor.transpose(flipped[:, b * P : (b + 1) * P], rows[c][:, b, :], identity[:])
+            flipped = psum.tile([P, P // 2, RUN, 2], BF16, name="flipped", tag="bank")
+            for r in range(RUN):
+                nc.tensor.transpose(flipped[:, :, r, :], rows[c][:, r, :], identity[:])
+            in_order = window[:, c * CHUNK : (c + 1) * CHUNK].rearrange("e (h l r) -> e h l r", l=2, r=RUN)
             if c % 2 == 0:
-                nc.vector.tensor_copy(window[:, c * CHUNK : (c + 1) * CHUNK], flipped[:])
+                nc.vector.tensor_copy(in_order, flipped[:].rearrange("e h r l -> e h l r"))
             else:
-                nc.scalar.copy(window[:, c * CHUNK : (c + 1) * CHUNK], flipped[:])
-                nc.tensor.matmul(unread_ps[:], identity[:], rows[c][:].rearrange("p b e -> p (b e)"), start=True, stop=True)
+                nc.scalar.copy(in_order, flipped[:].rearrange("e h r l -> e h l r"))
+                nc.tensor.matmul(unread_ps[:], identity[:], rows[c][:].rearrange("p r e -> p (r e)"), start=True, stop=True)
 
 
         root_bf = {}

@@ -29,14 +29,14 @@ def tile_boenet_kernel(tc, table, w, proj_b, child_w, child_b, sib_emb, head_w, 
         work = ctx.enter_context(tc.tile_pool(name="work", bufs=1))
         psum = ctx.enter_context(tc.psum_pool(name="psum", bufs=7))
 
-        identity = held.tile([P, P], BF16, name="identity")
-        make_identity(nc, identity[:])
-
         unread_ps = psum.tile([P, N], F32, name="unread_ps", bufs=1)
         zeros = held.tile([P, N], BF16, name="zeros")
-        nc.vector.memset(zeros[:], 0.0)
+        nc.gpsimd.memset(zeros[:], 0.0)
         for i in range(WARM_UP):
             nc.tensor.matmul(unread_ps[:], zeros[:, 0:P], zeros[:], start=True, stop=True)
+
+        identity = held.tile([P, P], BF16, name="identity")
+        make_identity(nc, identity[:])
 
         rows = []
         for c in range(CHUNKS):
@@ -56,9 +56,9 @@ def tile_boenet_kernel(tc, table, w, proj_b, child_w, child_b, sib_emb, head_w, 
         head_sb = held.tile([P, HALVES, O], BF16, name="head_sb")
         head_bias = held.tile([P, OUT_BLOCKS], F32, name="head_bias")
         with nc.allow_non_contiguous_dma(reason="bias vectors, one element to a partition"):
+            nc.sync.dma_start(w_sb[:], w)
             nc.sync.dma_start(proj_bias[:], proj_b.rearrange("(a p) x -> p (a x)", p=P))
             nc.sync.dma_start(siblings[:], sib_emb.rearrange("(a p) k -> p a k", p=P))
-            nc.sync.dma_start(w_sb[:], w)
             nc.sync.dma_start(child_sb[:], child_w.rearrange("(a p) m -> p a m", p=P))
             nc.sync.dma_start(child_bias[:], child_b.rearrange("(a p) x -> p (a x)", p=P))
             nc.sync.dma_start(head_sb[:], head_w.rearrange("(a p) o -> p a o", p=P))
@@ -87,26 +87,28 @@ def tile_boenet_kernel(tc, table, w, proj_b, child_w, child_b, sib_emb, head_w, 
                 nc.tensor.matmul(unread_ps[:], identity[:], rows[c][:].rearrange("p r e -> p (r e)"), start=True, stop=True)
 
 
+        root_ps = {}
         root_bf = {}
-        root_part = {}
         for j in range(PIECES):
             for a in range(HALVES):
                 looked_up = window[:].indirect(offsets[:, j * PIECE // 16 : (j + 1) * PIECE // 16])
-                root_ps = psum.tile([P, PIECE], F32, name="root_ps", tag="bank")
-                nc.tensor.matmul(root_ps[:], w_sb[:, a * P : (a + 1) * P], looked_up, start=True, stop=True)
+                product = psum.tile([P, PIECE], F32, name="product", tag="bank")
+                nc.tensor.matmul(product[:], w_sb[:, a * P : (a + 1) * P], looked_up, start=True, stop=True)
                 h_bf = work.tile([P, PIECE], BF16, name=f"h_bf_{a}_{j}")
-                h_part = work.tile([P, PIECE], F32, name=f"h_part_{a}_{j}")
                 if a == 0:
-                    nc.vector.tensor_scalar(h_bf[:], root_ps[:], proj_bias[:, a : a + 1], None, ADD)
-                    nc.vector.tensor_scalar(h_part[:], root_ps[:], MEAN, root_bias[:, a : a + 1], MULT, ADD)
+                    nc.vector.tensor_scalar(h_bf[:], product[:], proj_bias[:, a : a + 1], None, ADD)
                 else:
-                    nc.scalar.activation(h_bf[:], root_ps[:], FUNC.Identity, bias=proj_bias[:, a : a + 1])
-                    nc.scalar.activation(h_part[:], root_ps[:], FUNC.Identity, bias=root_bias[:, a : a + 1], scale=MEAN)
+                    nc.scalar.activation(h_bf[:], product[:], FUNC.Identity, bias=proj_bias[:, a : a + 1])
+                root_ps[a, j] = product
                 root_bf[a, j] = h_bf
-                root_part[a, j] = h_part
 
         pooled = {}
         for j in range(PIECES):
+            root_part = {}
+            for a in range(HALVES):
+                h_part = work.tile([P, PIECE], F32, name=f"h_part_{a}_{j}")
+                nc.vector.tensor_scalar(h_part[:], root_ps[a, j][:], MEAN, root_bias[:, a : a + 1], MULT, ADD)
+                root_part[a] = h_part
             for m in range(HALVES):
                 child_ps = psum.tile([P, PIECE], F32, name="child_ps", tag="bank")
                 for a in range(HALVES):
@@ -114,7 +116,7 @@ def tile_boenet_kernel(tc, table, w, proj_b, child_w, child_b, sib_emb, head_w, 
                 child = work.tile([P, PIECE], F32, name=f"child_{m}_{j}")
                 nc.scalar.activation(child[:], child_ps[:], FUNC.Tanh, bias=child_bias[:, m : m + 1])
                 mean_bf = work.tile([P, PIECE], BF16, name=f"mean_bf_{m}_{j}")
-                nc.vector.scalar_tensor_tensor(mean_bf[:], child[:], 2.0 * MEAN, root_part[m, j][:], MULT, ADD)
+                nc.vector.scalar_tensor_tensor(mean_bf[:], child[:], 2.0 * MEAN, root_part[m][:], MULT, ADD)
                 pooled[m, j] = mean_bf
 
         for j in range(PIECES):

@@ -30,10 +30,10 @@ def tile_boenet_kernel(tc, table, w, proj_b, child_w, child_b, sib_emb, head_w, 
         psum = ctx.enter_context(tc.psum_pool(name="psum", bufs=7))
 
         unread_ps = psum.tile([P, N], F32, name="unread_ps", bufs=1)
-        zeros = held.tile([P, N], BF16, name="zeros")
-        nc.gpsimd.memset(zeros[:], 0.0)
+        zero = held.tile([P, 1], BF16, name="zero")
+        nc.vector.memset(zero[:], 0.0)
         for i in range(WARM_UP):
-            nc.tensor.matmul(unread_ps[:], zeros[:, 0:P], zeros[:], start=True, stop=True)
+            nc.tensor.matmul(unread_ps[:], zero[:].to_broadcast([P, P]), zero[:].to_broadcast([P, N]), start=True, stop=True)
 
         identity = held.tile([P, P], BF16, name="identity")
         make_identity(nc, identity[:])

@@ -19,6 +19,7 @@ RUN = CHUNK // P
 PIECE = 256
 PIECES = N // PIECE
 WARM_UP = 4
+KEEP_UP = 3
 MEAN = 1.0 / (3.0 + 1e-8)
 
 
@@ -84,7 +85,8 @@ def tile_boenet_kernel(tc, table, w, proj_b, child_w, child_b, sib_emb, head_w, 
                 nc.vector.tensor_copy(in_order, flipped[:].rearrange("e h r l -> e h l r"))
             else:
                 nc.scalar.copy(in_order, flipped[:].rearrange("e h r l -> e h l r"))
-                nc.tensor.matmul(unread_ps[:], identity[:], rows[c][:].rearrange("p r e -> p (r e)"), start=True, stop=True)
+                for i in range(KEEP_UP if c == CHUNKS - 1 else 1):
+                    nc.tensor.matmul(unread_ps[:], identity[:], rows[c][:].rearrange("p r e -> p (r e)"), start=True, stop=True)
 
 
         root_ps = {}

@@ -16,8 +16,7 @@ OUT_BLOCKS = O // P
 CHUNK = 512
 CHUNKS = V // CHUNK
 RUN = CHUNK // P
-PIECE = 256
-PIECES = N // PIECE
+PIECES = ((0, 224), (224, 288))
 WARM_UP = 4
 KEEP_UP = 3
 MEAN = 1.0 / (3.0 + 1e-8)
@@ -91,12 +90,12 @@ def tile_boenet_kernel(tc, table, w, proj_b, child_w, child_b, sib_emb, head_w, 
 
         root_ps = {}
         root_bf = {}
-        for j in range(PIECES):
+        for j, (first, width) in enumerate(PIECES):
             for a in range(HALVES):
-                looked_up = window[:].indirect(offsets[:, j * PIECE // 16 : (j + 1) * PIECE // 16])
-                product = psum.tile([P, PIECE], F32, name="product", tag="bank")
+                looked_up = window[:].indirect(offsets[:, first // 16 : (first + width) // 16])
+                product = psum.tile([P, width], F32, name="product", tag="bank")
                 nc.tensor.matmul(product[:], w_sb[:, a * P : (a + 1) * P], looked_up, start=True, stop=True)
-                h_bf = work.tile([P, PIECE], BF16, name=f"h_bf_{a}_{j}")
+                h_bf = work.tile([P, width], BF16, name=f"h_bf_{a}_{j}")
                 if a == 0:
                     nc.vector.tensor_scalar(h_bf[:], product[:], proj_bias[:, a : a + 1], None, ADD)
                 else:
@@ -105,30 +104,30 @@ def tile_boenet_kernel(tc, table, w, proj_b, child_w, child_b, sib_emb, head_w, 
                 root_bf[a, j] = h_bf
 
         pooled = {}
-        for j in range(PIECES):
+        for j, (first, width) in enumerate(PIECES):
             root_part = {}
             for a in range(HALVES):
-                h_part = work.tile([P, PIECE], F32, name=f"h_part_{a}_{j}")
+                h_part = work.tile([P, width], F32, name=f"h_part_{a}_{j}")
                 nc.vector.tensor_scalar(h_part[:], root_ps[a, j][:], MEAN, root_bias[:, a : a + 1], MULT, ADD)
                 root_part[a] = h_part
             for m in range(HALVES):
-                child_ps = psum.tile([P, PIECE], F32, name="child_ps", tag="bank")
+                child_ps = psum.tile([P, width], F32, name="child_ps", tag="bank")
                 for a in range(HALVES):
                     nc.tensor.matmul(child_ps[:], child_sb[:, a, m * P : (m + 1) * P], root_bf[a, j][:], start=(a == 0), stop=(a == HALVES - 1))
-                child = work.tile([P, PIECE], F32, name=f"child_{m}_{j}")
+                child = work.tile([P, width], F32, name=f"child_{m}_{j}")
                 nc.scalar.activation(child[:], child_ps[:], FUNC.Tanh, bias=child_bias[:, m : m + 1])
-                mean_bf = work.tile([P, PIECE], BF16, name=f"mean_bf_{m}_{j}")
+                mean_bf = work.tile([P, width], BF16, name=f"mean_bf_{m}_{j}")
                 nc.vector.scalar_tensor_tensor(mean_bf[:], child[:], 2.0 * MEAN, root_part[m][:], MULT, ADD)
                 pooled[m, j] = mean_bf
 
-        for j in range(PIECES):
+        for j, (first, width) in enumerate(PIECES):
             for o in range(OUT_BLOCKS):
-                head_ps = psum.tile([P, PIECE], F32, name="head_ps", tag="bank")
+                head_ps = psum.tile([P, width], F32, name="head_ps", tag="bank")
                 for m in range(HALVES):
                     nc.tensor.matmul(head_ps[:], head_sb[:, m, o * P : (o + 1) * P], pooled[m, j][:], start=(m == 0), stop=(m == HALVES - 1))
-                logits = work.tile([P, PIECE], F32, name=f"logits_{o}_{j}")
-                if o % 2 == 0:
+                logits = work.tile([P, width], F32, name=f"logits_{o}_{j}")
+                if o % 2 == 1:
                     nc.vector.tensor_scalar(logits[:], head_ps[:], head_bias[:, o : o + 1], None, ADD)
                 else:
                     nc.scalar.activation(logits[:], head_ps[:], FUNC.Identity, bias=head_bias[:, o : o + 1])
-                nc.sync.dma_start(out[o * P : (o + 1) * P, j * PIECE : (j + 1) * PIECE], logits[:])
+                nc.sync.dma_start(out[o * P : (o + 1) * P, first : first + width], logits[:])

from contextlib import ExitStack

import concourse.mybir as mybir
from concourse.masks import make_identity

V, E, H, O, N = 4096, 128, 256, 512, 512
P = 128
FLOPS = 2 * N * (E * H + H * H + H * O)

BF16, F32, U16 = mybir.dt.bfloat16, mybir.dt.float32, mybir.dt.uint16
ADD, MULT = mybir.AluOpType.add, mybir.AluOpType.mult
FUNC = mybir.ActivationFunctionType

HALVES = H // P
OUT_BLOCKS = O // P
CHUNK = 512
CHUNKS = V // CHUNK
RUN = CHUNK // P
PIECES = ((0, 224), (224, 288))
WARM_UP = 4
KEEP_UP = 3
MEAN = 1.0 / (3.0 + 1e-8)


def tile_boenet_kernel(tc, table, w, proj_b, child_w, child_b, sib_emb, head_w, head_b, offs, out):
    nc = tc.nc
    with ExitStack() as ctx:
        held = ctx.enter_context(tc.tile_pool(name="held", bufs=1))
        work = ctx.enter_context(tc.tile_pool(name="work", bufs=1))
        psum = ctx.enter_context(tc.psum_pool(name="psum", bufs=7))

        unread_ps = psum.tile([P, N], F32, name="unread_ps", bufs=1)
        zero = held.tile([P, 1], BF16, name="zero")
        nc.vector.memset(zero[:], 0.0)
        for i in range(WARM_UP):
            nc.tensor.matmul(unread_ps[:], zero[:].to_broadcast([P, P]), zero[:].to_broadcast([P, N]), start=True, stop=True)

        identity = held.tile([P, P], BF16, name="identity")
        make_identity(nc, identity[:])

        rows = []
        for c in range(CHUNKS):
            chunk = held.tile([P, RUN, E], BF16, name=f"rows{c}")
            queue = nc.sync if c % 2 == 0 else nc.scalar
            queue.dma_start(chunk[:], table[c * CHUNK : (c + 1) * CHUNK, :].rearrange("(p r) e -> p r e", r=RUN))
            rows.append(chunk)

        offsets = held.tile([P, N // 16], U16, name="offsets")
        nc.sync.dma_start(offsets[:], offs)

        proj_bias = held.tile([P, HALVES], F32, name="proj_bias")
        siblings = held.tile([P, HALVES, 2], F32, name="siblings")
        w_sb = held.tile([P, H], BF16, name="w_sb")
        child_sb = held.tile([P, HALVES, H], BF16, name="child_sb")
        child_bias = held.tile([P, HALVES], F32, name="child_bias")
        head_sb = held.tile([P, HALVES, O], BF16, name="head_sb")
        head_bias = held.tile([P, OUT_BLOCKS], F32, name="head_bias")
        with nc.allow_non_contiguous_dma(reason="bias vectors, one element to a partition"):
            nc.sync.dma_start(w_sb[:], w)
            nc.sync.dma_start(proj_bias[:], proj_b.rearrange("(a p) x -> p (a x)", p=P))
            nc.sync.dma_start(siblings[:], sib_emb.rearrange("(a p) k -> p a k", p=P))
            nc.sync.dma_start(child_sb[:], child_w.rearrange("(a p) m -> p a m", p=P))
            nc.sync.dma_start(child_bias[:], child_b.rearrange("(a p) x -> p (a x)", p=P))
            nc.sync.dma_start(head_sb[:], head_w.rearrange("(a p) o -> p a o", p=P))
            nc.sync.dma_start(head_bias[:], head_b.rearrange("(a p) x -> p (a x)", p=P))

        warm = held.tile([P, 1], F32, name="warm")
        nc.vector.memset(warm[:], 0.0)
        nc.scalar.activation(warm[:], warm[:], FUNC.Tanh)

        root_bias = held.tile([P, HALVES], F32, name="root_bias")
        nc.gpsimd.tensor_tensor(root_bias[:], siblings[:, :, 0], siblings[:, :, 1], ADD)
        nc.gpsimd.tensor_scalar(root_bias[:], root_bias[:], 1.0 / 16.0, None, MULT)
        nc.gpsimd.tensor_tensor(root_bias[:], root_bias[:], proj_bias[:], ADD)
        nc.gpsimd.tensor_scalar(root_bias[:], root_bias[:], MEAN, None, MULT)

        window = held.tile([P, V], BF16, name="window")
        for c in range(CHUNKS):
            flipped = psum.tile([P, P // 2, RUN, 2], BF16, name="flipped", tag="bank")
            for r in range(RUN):
                nc.tensor.transpose(flipped[:, :, r, :], rows[c][:, r, :], identity[:])
            in_order = window[:, c * CHUNK : (c + 1) * CHUNK].rearrange("e (h l r) -> e h l r", l=2, r=RUN)
            if c % 2 == 0:
                nc.vector.tensor_copy(in_order, flipped[:].rearrange("e h r l -> e h l r"))
            else:
                nc.scalar.copy(in_order, flipped[:].rearrange("e h r l -> e h l r"))
                for i in range(KEEP_UP if c == CHUNKS - 1 else 1):
                    nc.tensor.matmul(unread_ps[:], identity[:], rows[c][:].rearrange("p r e -> p (r e)"), start=True, stop=True)


        root_ps = {}
        root_bf = {}
        for j, (first, width) in enumerate(PIECES):
            for a in range(HALVES):
                looked_up = window[:].indirect(offsets[:, first // 16 : (first + width) // 16])
                product = psum.tile([P, width], F32, name="product", tag="bank")
                nc.tensor.matmul(product[:], w_sb[:, a * P : (a + 1) * P], looked_up, start=True, stop=True)
                h_bf = work.tile([P, width], BF16, name=f"h_bf_{a}_{j}")
                if a == 0:
                    nc.vector.tensor_scalar(h_bf[:], product[:], proj_bias[:, a : a + 1], None, ADD)
                else:
                    nc.scalar.activation(h_bf[:], product[:], FUNC.Identity, bias=proj_bias[:, a : a + 1])
                root_ps[a, j] = product
                root_bf[a, j] = h_bf

        pooled = {}
        for j, (first, width) in enumerate(PIECES):
            root_part = {}
            for a in range(HALVES):
                h_part = work.tile([P, width], F32, name=f"h_part_{a}_{j}")
                nc.vector.tensor_scalar(h_part[:], root_ps[a, j][:], MEAN, root_bias[:, a : a + 1], MULT, ADD)
                root_part[a] = h_part
            for m in range(HALVES):
                child_ps = psum.tile([P, width], F32, name="child_ps", tag="bank")
                for a in range(HALVES):
                    nc.tensor.matmul(child_ps[:], child_sb[:, a, m * P : (m + 1) * P], root_bf[a, j][:], start=(a == 0), stop=(a == HALVES - 1))
                child = work.tile([P, width], F32, name=f"child_{m}_{j}")
                nc.scalar.activation(child[:], child_ps[:], FUNC.Tanh, bias=child_bias[:, m : m + 1])
                mean_bf = work.tile([P, width], BF16, name=f"mean_bf_{m}_{j}")
                nc.vector.scalar_tensor_tensor(mean_bf[:], child[:], 2.0 * MEAN, root_part[m][:], MULT, ADD)
                pooled[m, j] = mean_bf

        for j, (first, width) in enumerate(PIECES):
            for o in range(OUT_BLOCKS):
                head_ps = psum.tile([P, width], F32, name="head_ps", tag="bank")
                for m in range(HALVES):
                    nc.tensor.matmul(head_ps[:], head_sb[:, m, o * P : (o + 1) * P], pooled[m, j][:], start=(m == 0), stop=(m == HALVES - 1))
                logits = work.tile([P, width], F32, name=f"logits_{o}_{j}")
                if o % 2 == 1:
                    nc.vector.tensor_scalar(logits[:], head_ps[:], head_bias[:, o : o + 1], None, ADD)
                else:
                    nc.scalar.activation(logits[:], head_ps[:], FUNC.Identity, bias=head_bias[:, o : o + 1])
                nc.sync.dma_start(out[o * P : (o + 1) * P, first : first + width], logits[:])
